import numpy as np
import ml_dtypes

BF16 = ml_dtypes.bfloat16


def bf(x):
    return np.asarray(x, np.float32).astype(BF16)


def f32(x):
    return np.asarray(x, np.float32)


def f64(x):
    return np.asarray(x).astype(np.float64)


def striped(idx):
    return np.tile(idx.reshape(-1, 16).T, (8, 1))


D, S, N, M = 128, 256, 128, 512


def setup_inputs():
    return {
        'pe': bf(np.random.standard_normal((D, S))),
        'hid': bf(np.random.standard_normal((D, N))),
        'w2': bf(np.random.standard_normal((D, D)) * np.sqrt(2.0 / D)),
        'b2': f32(0.1 * np.random.standard_normal((D, 1))),
        'wqkv': bf(np.random.standard_normal((D, M - D)) / np.sqrt(D)),
        'bqkv': f32(0.1 * np.random.standard_normal((M - D, 1))),
        'offs': striped(np.random.permutation(np.tile(np.arange(S), 2))[:N]),
    }


def reference(pe, hid, w2, b2, wqkv, bqkv, offs):
    idx = offs[:16].T.reshape(-1)
    xin = f64(w2).T @ np.maximum(f64(hid), 0.0) + f64(b2)
    x = xin + f64(pe)[:, idx]
    return np.concatenate([f64(wqkv).T @ x + f64(bqkv), x], axis=0)

@@ -1,0 +1,87 @@
+import concourse.mybir as mybir
+
+BF16, F32, U16 = mybir.dt.bfloat16, mybir.dt.float32, mybir.dt.uint16
+ADD, MULT, IS_EQUAL = mybir.AluOpType.add, mybir.AluOpType.mult, mybir.AluOpType.is_equal
+IDENTITY = mybir.ActivationFunctionType.Identity
+
+P = 128
+AGENTS = 256
+TOKENS = 128
+QKV_BLOCKS = 3
+BLOCK = 32
+
+FLOPS = 2 * P * TOKENS * (P + QKV_BLOCKS * P)
+
+
+def tile_reltok_kernel(tc, pe, hid, w2, b2, wqkv, bqkv, offs, out):
+    nc = tc.nc
+    with (
+        tc.tile_pool(name="held", bufs=1) as held,
+        tc.psum_pool(name="banks", bufs=1) as banks,
+    ):
+        offsets = held.tile([P, TOKENS // 16], U16, name="offsets")
+        hid_sb = held.tile([P, TOKENS], BF16, name="hid_sb")
+        w2_sb = held.tile([P, P], BF16, name="w2_sb")
+        pe_sb = held.tile([P, AGENTS], BF16, name="pe_sb")
+        wqkv_sb = held.tile([P, QKV_BLOCKS * P], BF16, name="wqkv_sb")
+        bias_rows = held.tile([P, (QKV_BLOCKS + 1) * BLOCK], F32, name="bias_rows", align_bytes=64)
+        bias_cols = held.tile([P, (QKV_BLOCKS + 1) * BLOCK], F32, name="bias_cols", align_bytes=64)
+        nc.gpsimd.memset(bias_rows[:], 0.0)
+        nc.sync.dma_start(hid_sb[:], hid)
+        nc.scalar.dma_start(w2_sb[:], w2)
+        nc.sync.dma_start(offsets[:], offs)
+        nc.scalar.dma_start(pe_sb[:], pe)
+        nc.sync.dma_start(wqkv_sb[:], wqkv)
+        nc.scalar.dma_start(
+            bias_rows[0:P:BLOCK, QKV_BLOCKS * BLOCK : (QKV_BLOCKS + 1) * BLOCK],
+            b2.rearrange("(q r) o -> q (r o)", r=BLOCK),
+        )
+        nc.sync.dma_start(
+            bias_rows[0:P:BLOCK, 0 : QKV_BLOCKS * BLOCK].rearrange("q (c r) -> q c r", r=BLOCK),
+            bqkv.rearrange("(c q r) o -> q c (r o)", c=QKV_BLOCKS, r=BLOCK),
+        )
+
+        ones = held.tile([P, P], F32, name="ones")
+        nc.vector.memset(ones[:], 1.0)
+        column_index = held.tile([P, P], F32, name="column_index")
+        nc.vector.tensor_tensor_scan(column_index[:], ones[:], ones[:], -1.0, MULT, ADD)
+        row_index = banks.tile([P, 1], F32, name="row_index")
+        nc.tensor.matmul(row_index[:], column_index[0:1, :], ones[0:1, 0:1], start=True, stop=True)
+        identity = held.tile([P, P], BF16, name="identity")
+        nc.vector.tensor_scalar(identity[:], column_index[:], row_index[:, 0:1], None, IS_EQUAL)
+
+        warmed = held.tile([P, 1], F32, name="warmed")
+        nc.scalar.activation(warmed[:], ones[:, 0:1], IDENTITY)
+
+        relu_hid = held.tile([P, TOKENS], BF16, name="relu_hid")
+        nc.vector.tensor_scalar_max(relu_hid[:], hid_sb[:], 0.0)
+        nc.vector.transpose(bias_cols[:], bias_rows[:])
+        b2_sb = bias_cols[:, QKV_BLOCKS * BLOCK : QKV_BLOCKS * BLOCK + 1]
+
+        xin_bank = banks.tile([P, TOKENS], F32, name="xin_bank")
+        x_bank = banks.tile([P, TOKENS], F32, name="x_bank")
+        qkv_banks = [banks.tile([P, TOKENS], F32, name=f"qkv_bank{c}") for c in range(QKV_BLOCKS)]
+
+        nc.tensor.matmul(xin_bank[:], w2_sb[:], relu_hid[:], start=True, stop=True)
+        nc.tensor.matmul(x_bank[:], w2_sb[:], relu_hid[:], start=True, stop=False)
+        xin_bf = held.tile([P, TOKENS], BF16, name="xin_bf")
+        nc.vector.tensor_scalar(xin_bf[:], xin_bank[:], b2_sb, None, ADD)
+
+        looked_up = pe_sb[:].indirect(offsets[:])
+        nc.tensor.matmul(x_bank[:], identity[:], looked_up, start=False, stop=True)
+        for c in range(QKV_BLOCKS):
+            nc.tensor.matmul(qkv_banks[c][:], wqkv_sb[:, c * P : (c + 1) * P], looked_up, start=True, stop=False)
+
+        x_sb = held.tile([P, TOKENS], F32, name="x_sb")
+        nc.scalar.activation(x_sb[:], x_bank[:], IDENTITY, bias=b2_sb)
+        nc.scalar.dma_start(out[QKV_BLOCKS * P : (QKV_BLOCKS + 1) * P, :], x_sb[:])
+
+        for c in range(QKV_BLOCKS):
+            nc.tensor.matmul(qkv_banks[c][:], wqkv_sb[:, c * P : (c + 1) * P], xin_bf[:], start=False, stop=True)
+            block_sb = held.tile([P, TOKENS], F32, name=f"block_sb{c}")
+            if c % 2 == 0:
+                nc.vector.tensor_scalar(block_sb[:], qkv_banks[c][:], bias_cols[:, c * BLOCK : c * BLOCK + 1], None, ADD)
+                nc.sync.dma_start(out[c * P : (c + 1) * P, :], block_sb[:])
+            else:
+                nc.scalar.activation(block_sb[:], qkv_banks[c][:], IDENTITY, bias=bias_cols[:, c * BLOCK : c * BLOCK + 1])
+                nc.scalar.dma_start(out[c * P : (c + 1) * P, :], block_sb[:])

@@ -30,8 +30,8 @@ def tile_reltok_kernel(tc, pe, hid, w2, b2, wqkv, bqkv, offs, out):
         nc.sync.dma_start(hid_sb[:], hid)
         nc.scalar.dma_start(w2_sb[:], w2)
         nc.sync.dma_start(offsets[:], offs)
-        nc.scalar.dma_start(pe_sb[:], pe)
-        nc.sync.dma_start(wqkv_sb[:], wqkv)
+        nc.scalar.dma_start(wqkv_sb[:], wqkv)
+        nc.sync.dma_start(pe_sb[:], pe)
         nc.scalar.dma_start(
             bias_rows[0:P:BLOCK, QKV_BLOCKS * BLOCK : (QKV_BLOCKS + 1) * BLOCK],
             b2.rearrange("(q r) o -> q (r o)", r=BLOCK),

import concourse.mybir as mybir

BF16, F32, U16 = mybir.dt.bfloat16, mybir.dt.float32, mybir.dt.uint16
ADD, MULT, IS_EQUAL = mybir.AluOpType.add, mybir.AluOpType.mult, mybir.AluOpType.is_equal
IDENTITY = mybir.ActivationFunctionType.Identity

P = 128
AGENTS = 256
TOKENS = 128
QKV_BLOCKS = 3
BLOCK = 32

FLOPS = 2 * P * TOKENS * (P + QKV_BLOCKS * P)


def tile_reltok_kernel(tc, pe, hid, w2, b2, wqkv, bqkv, offs, out):
    nc = tc.nc
    with (
        tc.tile_pool(name="held", bufs=1) as held,
        tc.psum_pool(name="banks", bufs=1) as banks,
    ):
        offsets = held.tile([P, TOKENS // 16], U16, name="offsets")
        hid_sb = held.tile([P, TOKENS], BF16, name="hid_sb")
        w2_sb = held.tile([P, P], BF16, name="w2_sb")
        pe_sb = held.tile([P, AGENTS], BF16, name="pe_sb")
        wqkv_sb = held.tile([P, QKV_BLOCKS * P], BF16, name="wqkv_sb")
        bias_rows = held.tile([P, (QKV_BLOCKS + 1) * BLOCK], F32, name="bias_rows", align_bytes=64)
        bias_cols = held.tile([P, (QKV_BLOCKS + 1) * BLOCK], F32, name="bias_cols", align_bytes=64)
        nc.gpsimd.memset(bias_rows[:], 0.0)
        nc.sync.dma_start(hid_sb[:], hid)
        nc.scalar.dma_start(w2_sb[:], w2)
        nc.sync.dma_start(offsets[:], offs)
        nc.scalar.dma_start(wqkv_sb[:], wqkv)
        nc.sync.dma_start(pe_sb[:], pe)
        nc.scalar.dma_start(
            bias_rows[0:P:BLOCK, QKV_BLOCKS * BLOCK : (QKV_BLOCKS + 1) * BLOCK],
            b2.rearrange("(q r) o -> q (r o)", r=BLOCK),
        )
        nc.sync.dma_start(
            bias_rows[0:P:BLOCK, 0 : QKV_BLOCKS * BLOCK].rearrange("q (c r) -> q c r", r=BLOCK),
            bqkv.rearrange("(c q r) o -> q c (r o)", c=QKV_BLOCKS, r=BLOCK),
        )

        ones = held.tile([P, P], F32, name="ones")
        nc.vector.memset(ones[:], 1.0)
        column_index = held.tile([P, P], F32, name="column_index")
        nc.vector.tensor_tensor_scan(column_index[:], ones[:], ones[:], -1.0, MULT, ADD)
        row_index = banks.tile([P, 1], F32, name="row_index")
        nc.tensor.matmul(row_index[:], column_index[0:1, :], ones[0:1, 0:1], start=True, stop=True)
        identity = held.tile([P, P], BF16, name="identity")
        nc.vector.tensor_scalar(identity[:], column_index[:], row_index[:, 0:1], None, IS_EQUAL)

        warmed = held.tile([P, 1], F32, name="warmed")
        nc.scalar.activation(warmed[:], ones[:, 0:1], IDENTITY)

        relu_hid = held.tile([P, TOKENS], BF16, name="relu_hid")
        nc.vector.tensor_scalar_max(relu_hid[:], hid_sb[:], 0.0)
        nc.vector.transpose(bias_cols[:], bias_rows[:])
        b2_sb = bias_cols[:, QKV_BLOCKS * BLOCK : QKV_BLOCKS * BLOCK + 1]

        xin_bank = banks.tile([P, TOKENS], F32, name="xin_bank")
        x_bank = banks.tile([P, TOKENS], F32, name="x_bank")
        qkv_banks = [banks.tile([P, TOKENS], F32, name=f"qkv_bank{c}") for c in range(QKV_BLOCKS)]

        nc.tensor.matmul(xin_bank[:], w2_sb[:], relu_hid[:], start=True, stop=True)
        nc.tensor.matmul(x_bank[:], w2_sb[:], relu_hid[:], start=True, stop=False)
        xin_bf = held.tile([P, TOKENS], BF16, name="xin_bf")
        nc.vector.tensor_scalar(xin_bf[:], xin_bank[:], b2_sb, None, ADD)

        looked_up = pe_sb[:].indirect(offsets[:])
        nc.tensor.matmul(x_bank[:], identity[:], looked_up, start=False, stop=True)
        for c in range(QKV_BLOCKS):
            nc.tensor.matmul(qkv_banks[c][:], wqkv_sb[:, c * P : (c + 1) * P], looked_up, start=True, stop=False)

        x_sb = held.tile([P, TOKENS], F32, name="x_sb")
        nc.scalar.activation(x_sb[:], x_bank[:], IDENTITY, bias=b2_sb)
        nc.scalar.dma_start(out[QKV_BLOCKS * P : (QKV_BLOCKS + 1) * P, :], x_sb[:])

        for c in range(QKV_BLOCKS):
            nc.tensor.matmul(qkv_banks[c][:], wqkv_sb[:, c * P : (c + 1) * P], xin_bf[:], start=False, stop=True)
            block_sb = held.tile([P, TOKENS], F32, name=f"block_sb{c}")
            if c % 2 == 0:
                nc.vector.tensor_scalar(block_sb[:], qkv_banks[c][:], bias_cols[:, c * BLOCK : c * BLOCK + 1], None, ADD)
                nc.sync.dma_start(out[c * P : (c + 1) * P, :], block_sb[:])
            else:
                nc.scalar.activation(block_sb[:], qkv_banks[c][:], IDENTITY, bias=bias_cols[:, c * BLOCK : c * BLOCK + 1])
                nc.scalar.dma_start(out[c * P : (c + 1) * P, :], block_sb[:])
